import numpy as np
import ml_dtypes


def mxq(x, axis, fmt="e4m3"):
    dtype, down = {"e4m3": (ml_dtypes.float8_e4m3fn, 7), "e5m2": (ml_dtypes.float8_e5m2, 14)}[fmt]
    v = np.moveaxis(np.asarray(x, np.float32).astype(ml_dtypes.bfloat16).astype(np.float64), axis, -1)
    blocks = v.reshape(v.shape[:-1] + (-1, 32))
    amax = np.abs(blocks).max(-1, keepdims=True)
    byte = np.maximum(np.where(amax > 0, np.frexp(amax)[1] - 1 + 127, 0) - down, 1)
    scale = np.exp2(byte - 127.0)
    codes = (blocks / scale).astype(np.float32).astype(dtype).astype(np.float64)
    return np.moveaxis((codes * scale).reshape(v.shape), -1, axis)


WIDE = False


def mx_kscale(k):
    if not WIDE:
        return np.ones(k)
    levels = np.array([10, -10, 5, -5, 0])
    if k % 512:
        return np.exp2(np.random.permutation(np.resize(levels, k // 32))).repeat(32)
    a = np.empty((k // 512, 16))
    for p in range(k // 512):
        a[p, :8] = np.random.permutation(np.resize(levels, 8))
        for g in range(8):
            far = levels[np.abs(levels - a[p, g]) >= 10]
            a[p, g + 8] = far[np.random.randint(len(far))]
    return np.exp2(a.ravel()).repeat(32)


BF16 = ml_dtypes.bfloat16


def bf(x):
    return np.asarray(x, np.float32).astype(BF16)


def f64(x):
    return np.asarray(x).astype(np.float64)


B, S, DV, D, H, A = 2, 256, 1024, 1024, 8, 64
LN_EPS = 1e-3


def setup_inputs():
    s = mx_kscale(DV)
    return {
        "attn": bf(np.random.standard_normal((B, H, S, DV)) * 0.4 * s),
        "Wo": bf(np.random.standard_normal((H, DV, D)) * 0.6 / np.sqrt(DV * H) / s[None, :, None]),
        "bo": bf(np.random.standard_normal((H, D)) * 0.12 / np.sqrt(H)),
        "query_inputs": bf(np.random.standard_normal((B, S, D)) * 0.1),
        "gamma": bf(1.0 + 0.1 * np.random.standard_normal(D)),
        "beta": bf(0.1 * np.random.standard_normal(D)),
    }


def core(attn, Wo, bo, query_inputs, gamma, beta):
    pre = mxq(f64(attn), 3, "e4m3") @ mxq(f64(Wo), 1, "e4m3")
    head_out = np.maximum(pre + f64(bo)[None, :, None, :], 0.0)
    x = f64(query_inputs) + head_out.sum(axis=1)
    mean = x.mean(axis=-1, keepdims=True)
    var = x.var(axis=-1, keepdims=True)
    return f64(gamma) * (x - mean) / np.sqrt(var + LN_EPS) + f64(beta)


def e4m3fn_bytes(y):
    return np.clip(np.asarray(y, np.float64), -448.0, 448.0).astype(np.float32).astype(ml_dtypes.float8_e4m3fn).view(np.uint8)


def reference(attn, Wo, bo, query_inputs, gamma, beta):
    out = core(attn, Wo, bo, query_inputs, gamma, beta)
    s = np.max(np.abs(out)) / 448.0
    return out, e4m3fn_bytes(out / s)

@@ -1,0 +1,495 @@
+from contextlib import ExitStack
+
+import concourse.mybir as mybir
+from concourse.masks import make_identity
+
+B, H, S, DV, D = 2, 8, 256, 1024, 1024
+LN_EPS = 1e-3
+FLOPS = 2 * B * H * S * DV * D
+
+F32 = mybir.dt.float32
+BF16 = mybir.dt.bfloat16
+U32 = mybir.dt.uint32
+U8 = mybir.dt.uint8
+FP8X4 = mybir.dt.float8_e4m3fn_x4
+FP8 = mybir.dt.float8_e4m3fn
+ALU = mybir.AluOpType
+ACT = mybir.ActivationFunctionType
+AX = mybir.AxisListType
+
+P = 128
+NT = B * S
+R = NT // P
+NG = DV // 512
+HD = D // 2
+NU = 2 * H
+GC = 384
+VA = (352, 176)
+VB = (352, 384)
+VA2 = 416
+ABUFS = 3
+WBUFS = 6
+PRE = 3
+LE = 3
+
+
+def tile_multiheadattentionunit_pa_kernel(tc, attn, Wo, bo, query_inputs, gamma, beta, out_0, out_1):
+    nc = tc.nc
+    with ExitStack() as ctx:
+        const = ctx.enter_context(tc.tile_pool(name="const", bufs=1))
+        stream = ctx.enter_context(tc.tile_pool(name="stream", bufs=2))
+        psum = ctx.enter_context(tc.psum_pool(name="psum", bufs=4))
+        ctx.enter_context(tc.manual_schedule())
+
+        araws = {}
+        wraws = {}
+
+        def load_attn(h):
+            araw = stream.tile([P, R, DV], BF16, tag="araw", bufs=ABUFS, name="araw")
+            nc.sync.dma_start(
+                out=araw[:].rearrange("p (b e) k -> p b (e k)", b=B),
+                in_=attn[:, h].rearrange("b (p e) k -> p b (e k)", e=2),
+            )
+            for g in range(NG):
+                araws[(h, g)] = araw[:, :, 512 * g : 512 * (g + 1)]
+
+        def load_wo(h, g):
+            wraw = stream.tile([P, 4, D], BF16, tag="wraw", bufs=WBUFS, name="wraw")
+            nc.sync.dma_start(
+                out=wraw[:], in_=Wo[h, 512 * g : 512 * (g + 1), :].rearrange("(p j) d -> p j d", j=4)
+            )
+            for hf in range(2):
+                wraws[(h, g, hf)] = wraw[:, :, hf * HD : (hf + 1) * HD]
+
+        def loads(h):
+            load_attn(h)
+            for g in ((1, 0) if h == 1 else (0, 1)):
+                load_wo(h, g)
+
+        one = const.tile([P, 1], F32, name="one")
+        nc.vector.memset(one[:], 1.0)
+        zero = const.tile([P, 1], F32, name="zero")
+        nc.vector.memset(zero[:], 0.0)
+        warm = const.tile([P, 1], F32, name="warm")
+        nc.scalar.activation(out=warm[:], in_=one[:], func=ACT.Sqrt)
+
+        braw = const.tile([P, P], BF16, name="braw")
+        nc.vector.memset(braw[64:128, :], 0.0)
+        nc.scalar.dma_start(out=braw[0:64, :], in_=bo.rearrange("h (c p) -> (h c) p", p=P))
+
+        for h in range(PRE):
+            loads(h)
+
+        ident_b = const.tile([P, P], BF16, name="ident_b")
+        make_identity(nc, ident_b[:])
+        ident_f = const.tile([P, P], F32, name="ident_f")
+        make_identity(nc, ident_f[:])
+
+        NDC = D // P
+        bT = psum.tile([P, P], BF16, tag="tp", bufs=4, name="bT")
+        nc.tensor.transpose(bT[:], braw[:], ident_b[:])
+        negb = const.tile([P, H * NDC], F32, name="negb")
+        nc.vector.tensor_scalar(out=negb[:], in0=bT[:, 0 : H * NDC], scalar1=-1.0, scalar2=None, op0=ALU.mult)
+        posb = const.tile([P, H * NDC], F32, name="posb")
+        nc.vector.tensor_copy(out=posb[:], in_=bT[:, 0 : H * NDC])
+        bsum = const.tile([P, NDC], F32, name="bsum")
+        nc.vector.tensor_reduce(
+            out=bsum[:], in_=posb[:].rearrange("p (h c) -> p c h", h=H), axis=AX.X, op=ALU.add
+        )
+
+        qraw = const.tile([P, R, D], BF16, name="qraw")
+        gam = const.tile([P, D], BF16, name="gam")
+        bet = const.tile([P, D], BF16, name="bet")
+
+        tps = {}
+        agrps = {}
+        acodes = {}
+        wgrps = {}
+        wcodes = {}
+        mms = {}
+
+        def attn_T(a):
+            if a >= NU:
+                return
+            h, g = a // 2, a % 2
+            araw = araws[(h, g)]
+            for r2 in range(2):
+                tp = psum.tile([P, 2, 2, P], F32, tag="tp", bufs=4, name="tp")
+                for rr in range(2):
+                    words = araw[:, 2 * r2 + rr, :].bitcast(F32)
+                    for u in range(2):
+                        nc.tensor.transpose(tp[:, rr, u, :], words[:, u:256:2], ident_f[:])
+                tps[(a, r2)] = tp
+
+        def attn_E(a):
+            if a >= NU:
+                return
+            h, g = a // 2, a % 2
+            if g == 0:
+                agrp = stream.tile([P, NG, 4 * NT], BF16, tag="agrp", bufs=2, name="agrp", align_bytes=64)
+                agrps[h] = agrp
+            gw = agrps[h][:, g, :].bitcast(F32).rearrange("p (r n u) -> p r n u", r=R, u=2)
+            for r2 in range(2):
+                nc.scalar.copy(
+                    out=gw[:, 2 * r2 : 2 * r2 + 2, :, :], in_=tps[(a, r2)][:].rearrange("p r u n -> p r n u")
+                )
+
+        def attn_Q(h):
+            if h >= H:
+                return
+            code = stream.tile([P, NG, NT], U32, tag="acode", bufs=2, name="acode", align_bytes=64)
+            scl = stream.tile([P, NG, NT], U8, tag="ascl", bufs=2, name="ascl", align_bytes=64)
+            nc.vector.quantize_mx(
+                out=code[:].rearrange("p g n -> p (g n)").bitcast(FP8X4),
+                scales=scl[:].rearrange("p g n -> p (g n)"),
+                in_=agrps[h][:].rearrange("p g n -> p (g n)"),
+            )
+            acodes[h] = (code, scl)
+
+        def icopy(eng, k, g, lo, hi):
+            h, half = k // 2, k % 2
+            src = wraws[(h, g, half)][:, :, lo:hi].rearrange("p j d -> p d j")
+            dst = wgrps[(k, g)][:, lo:hi, :]
+            if eng == "V":
+                nc.vector.tensor_copy(out=dst, in_=src)
+            elif eng == "S":
+                nc.scalar.copy(
+                    out=wgrps[(k, g)][:, lo:hi, :].rearrange("p (c i) t -> p c t i", i=4),
+                    in_=wraws[(h, g, half)][:, :, lo:hi].rearrange("p t (c i) -> p c t i", i=4),
+                )
+            else:
+                nc.gpsimd.tensor_scalar(out=dst, in0=src, scalar1=1.0, scalar2=0.0, op0=ALU.mult, op1=ALU.add)
+
+        def wo_alloc(k, g):
+            if g == 0:
+                wgrpa = stream.tile([P, HD, 4], BF16, tag="wgrpa", bufs=2, name="wgrpa", align_bytes=64)
+                wgrps[(k, 0)] = wgrpa
+            else:
+                wgrpb = stream.tile([P, HD, 4], BF16, tag="wgrpb", bufs=1, name="wgrpb", align_bytes=64)
+                wgrps[(k, 1)] = wgrpb
+
+        def wo_Q(k):
+            if k >= NU:
+                return
+            code = stream.tile([P, NG, HD], U32, tag="wcode", bufs=3, name="wcode", align_bytes=64)
+            scl = stream.tile([P, NG, HD], U8, tag="wscl", bufs=3, name="wscl", align_bytes=64)
+            for g in range(NG):
+                nc.vector.quantize_mx(
+                    out=code[:, g, :].bitcast(FP8X4),
+                    scales=scl[:, g, :],
+                    in_=wgrps[(k, g)][:].rearrange("p d j -> p (d j)"),
+                )
+            wcodes[k] = (code, scl)
+
+        accs = []
+        for c in range(NDC):
+            acc = const.tile([P, NT], F32, name="acc%d" % c)
+            accs.append(acc)
+
+        def mx(k, i):
+            if k >= NU:
+                return
+            h = k // 2
+            mm = psum.tile([P, NT], F32, tag=("tp" if k == NU - 1 else "mm"), bufs=4, name="mm")
+            cols = slice(i * P, (i + 1) * P)
+            ac, asc = acodes[h]
+            wc, ws = wcodes[k]
+            for g in range(NG):
+                nc.tensor.matmul_mx(
+                    out=mm[:],
+                    lhsT=wc[:, g, cols].bitcast(FP8X4),
+                    lhsT_scale=ws[:, g, cols],
+                    rhs=ac[:, g, :].bitcast(FP8X4),
+                    rhs_scale=asc[:, g, :],
+                    start=(g == 0),
+                    stop=(g == NG - 1),
+                )
+            mms[(k, i)] = mm
+
+        def relu_add(k, i):
+            h, half = k // 2, k % 2
+            c = 4 * half + i
+            nb = negb[:, h * NDC + c : h * NDC + c + 1]
+            if h == 0:
+                nc.vector.tensor_scalar(
+                    out=accs[c][:], in0=mms[(k, i)][:], scalar1=nb, scalar2=bsum[:, c : c + 1],
+                    op0=ALU.max, op1=ALU.add,
+                )
+            else:
+                nc.vector.scalar_tensor_tensor(
+                    out=accs[c][:], in0=mms[(k, i)][:], scalar=nb, in1=accs[c][:], op0=ALU.max, op1=ALU.add
+                )
+
+        xts = {}
+
+        def x_open(r, hf):
+            xt = psum.tile([P, HD], F32, tag=("mm" if r < 2 else "tp"), bufs=4, name="xt%d%d" % (r, hf))
+            nc.tensor.matmul(
+                out=xt[:], lhsT=ident_b[:], rhs=qraw[:, r, hf * HD : (hf + 1) * HD], start=True, stop=False
+            )
+            xts[(r, hf)] = xt
+
+        def x_add(r, c):
+            nc.tensor.matmul(
+                out=xts[(r, c // 4)][:, (c % 4) * P : (c % 4 + 1) * P],
+                lhsT=accs[c][:, r * P : (r + 1) * P],
+                rhs=ident_f[:],
+                is_transpose=True,
+                start=False,
+                stop=(c % 4 == 3),
+            )
+
+        sts = []
+        for r in range(R):
+            st = const.tile([P, 8], F32, name="st%d" % r)
+            sts.append(st)
+
+        def s_sum(r, hf):
+            junk = stream.tile([P, HD], F32, tag="junk", bufs=2, name="junk")
+            nc.scalar.activation(
+                out=junk[:], in_=xts[(r, hf)][:], func=ACT.Identity, scale=-1.0 / D,
+                accum_out=sts[r][:, hf : hf + 1],
+            )
+
+        def s_negmean(r):
+            nc.scalar.activation(
+                out=sts[r][:, 2:3], in_=sts[r][:, 0:1], func=ACT.Identity, bias=sts[r][:, 1:2], scale=1.0
+            )
+
+        def s_square(r):
+            for hf in range(2):
+                junk = stream.tile([P, HD], F32, tag="junk", bufs=2, name="junk")
+                nc.scalar.activation(
+                    out=junk[:], in_=xts[(r, hf)][:], func=ACT.Square, bias=sts[r][:, 2:3], scale=1.0,
+                    accum_out=sts[r][:, 3 + hf : 4 + hf],
+                )
+
+        def v_stats(r):
+            bst = const.tile([P, 2, 6], F32, name="bst%d" % r)
+            for hf in range(2):
+                nc.vector.bn_stats(out=bst[:, hf, :], in_=xts[(r, hf)][:])
+            mv = const.tile([P, 2], F32, name="mv%d" % r)
+            nc.vector.bn_aggr(out=mv[:], in_=bst[:].rearrange("p a b -> p (a b)"))
+            mvs[r] = mv
+
+        def v_vareps_bn(r):
+            nc.vector.tensor_scalar(
+                out=sts[r][:, 5:6], in0=mvs[r][:, 1:2], scalar1=float(D), scalar2=LN_EPS * D,
+                op0=ALU.mult, op1=ALU.add,
+            )
+
+        def v_vareps(r):
+            nc.vector.tensor_scalar(
+                out=sts[r][:, 5:6], in0=sts[r][:, 3:4], scalar1=sts[r][:, 4:5], scalar2=LN_EPS * D,
+                op0=ALU.add, op1=ALU.add,
+            )
+
+        def s_sqrt(r):
+            nc.scalar.activation(out=sts[r][:, 6:7], in_=sts[r][:, 5:6], func=ACT.Sqrt, scale=1.0 / D)
+
+        def v_recip(r):
+            nc.vector.reciprocal(out=sts[r][:, 7:8], in_=sts[r][:, 6:7])
+
+        t1s = {}
+        ys = {}
+        mvs = {}
+        am = const.tile([P, R], F32, name="am")
+        o0v = out_0.rearrange("b (p e) d -> b p e d", e=2)
+        o1v = out_1.rearrange("b (p e) d -> b p e d", e=2)
+
+        def v_center_gain(r, hf):
+            if hf == 0:
+                t1 = stream.tile([P, D], F32, tag="t1", bufs=4, name="t1")
+                t1s[r] = t1
+            cols = slice(hf * HD, (hf + 1) * HD)
+            if r in mvs:
+                nc.vector.scalar_tensor_tensor(
+                    out=t1s[r][:, cols], in0=xts[(r, hf)][:], scalar=mvs[r][:, 0:1], in1=gam[:, cols],
+                    op0=ALU.subtract, op1=ALU.mult,
+                )
+            else:
+                nc.vector.scalar_tensor_tensor(
+                    out=t1s[r][:, cols], in0=xts[(r, hf)][:], scalar=sts[r][:, 2:3], in1=gam[:, cols],
+                    op0=ALU.add, op1=ALU.mult,
+                )
+
+        def v_scale_shift(r):
+            y = const.tile([P, D], F32, name="y%d" % r)
+            nc.vector.scalar_tensor_tensor(
+                out=y[:], in0=t1s[r][:], scalar=sts[r][:, 7:8], in1=bet[:], op0=ALU.mult, op1=ALU.add
+            )
+            nc.sync.dma_start(out=o0v[r // 2, :, r % 2, :], in_=y[:])
+            ys[r] = y
+
+        pm = const.tile([P, 1], F32, name="pm")
+
+        def v_prevmax():
+            nc.vector.tensor_reduce(out=pm[:], in_=am[:, 0 : R - 1], axis=AX.X, op=ALU.max)
+
+        def v_absmax(r):
+            nc.vector.tensor_reduce(
+                out=am[:, r : r + 1], in_=ys[r][:], axis=AX.X, op=ALU.max, apply_absolute_value=True
+            )
+
+        attn_T(0)
+        attn_T(1)
+        attn_E(0)
+        attn_E(1)
+        for k in range(2):
+            wo_alloc(k, 0)
+            icopy("V", k, 0, 0, VA[k])
+            icopy("S", k, 0, VA[k], HD)
+        attn_Q(0)
+        wo_alloc(0, 1)
+        icopy("V", 0, 1, 0, VB[0])
+        icopy("S", 0, 1, VB[0], HD)
+        wo_Q(0)
+        attn_T(2)
+        for i in range(4):
+            mx(0, i)
+        attn_T(3)
+        wo_alloc(1, 1)
+        icopy("V", 1, 1, 0, VB[1])
+        if VB[1] < HD:
+            icopy("S", 1, 1, VB[1], HD)
+        attn_E(2)
+
+        for s in range(NU):
+            if s % 2 == 0 and s // 2 + PRE < H:
+                loads(s // 2 + PRE)
+            if s == 10:
+                for b in range(B):
+                    nc.sync.dma_start(
+                        out=qraw[:, 2 * b : 2 * b + 2, :], in_=query_inputs[b].rearrange("(p e) d -> p e d", e=2)
+                    )
+                nc.sync.dma_start(out=gam[:], in_=gamma.partition_broadcast(P))
+                nc.sync.dma_start(out=bet[:], in_=beta.partition_broadcast(P))
+            wo_Q(s + 1)
+            if s == NU - 2:
+                for i in range(4):
+                    mx(s + 1, i)
+            k = s + 2
+            if k < NU:
+                wo_alloc(k, 0)
+                wo_alloc(k, 1)
+                icopy("G", k, 1, 0, GC)
+                if s == 0:
+                    icopy("S", k, 1, GC, HD)
+                    attn_E(s + LE)
+                    icopy("S", k, 0, VA2, HD)
+                else:
+                    icopy("S", k, 0, 0, HD)
+                    attn_E(s + LE)
+                    icopy("S", k, 1, GC, HD)
+            if s == NU - 1:
+                s_sum(1, 0)
+            for i in range(4):
+                relu_add(s, i)
+                if s < NU - 2:
+                    if i == 3:
+                        attn_T(s + LE + 1)
+                    mx(s + 1, i)
+                elif s == NU - 2:
+                    x_open(i // 2, i % 2)
+                    x_add(0, i)
+                    if i == 2:
+                        x_add(1, 0)
+                        x_add(1, 1)
+                    if i >= 2:
+                        x_add(1, i)
+                else:
+                    x_add(0, 4 + i)
+                    x_add(1, 4 + i)
+            if s % 2 == 0:
+                attn_Q(s // 2 + 1)
+            if s == 0:
+                icopy("V", k, 0, 0, VA2)
+
+        for r in range(2, R):
+            x_open(r, 0)
+            x_open(r, 1)
+            for c in range(NDC):
+                x_add(r, c)
+
+        v_stats(0)
+        v_vareps_bn(0)
+        s_sum(1, 1)
+        s_negmean(1)
+        s_sqrt(0)
+        v_center_gain(0, 0)
+        v_center_gain(0, 1)
+        s_sum(2, 0)
+        s_sum(2, 1)
+        s_negmean(2)
+        v_center_gain(1, 0)
+        v_recip(0)
+        v_center_gain(1, 1)
+        v_scale_shift(0)
+        s_square(1)
+        v_vareps(1)
+        s_sum(3, 0)
+        s_sqrt(1)
+        s_sum(3, 1)
+        s_negmean(3)
+        v_center_gain(2, 0)
+        v_recip(1)
+        v_center_gain(2, 1)
+        v_absmax(0)
+        v_scale_shift(1)
+        s_square(2)
+        v_vareps(2)
+        s_sqrt(2)
+        v_center_gain(3, 0)
+        v_recip(2)
+        v_center_gain(3, 1)
+        v_absmax(1)
+        v_scale_shift(2)
+        s_square(3)
+        v_vareps(3)
+        s_sqrt(3)
+        v_absmax(2)
+        v_prevmax()
+        v_recip(3)
+        v_scale_shift(3)
+        v_absmax(3)
+
+        amp = const.tile([P, 1], F32, name="amp")
+        nc.vector.tensor_scalar(
+            out=amp[:], in0=am[:, R - 1 : R], scalar1=pm[:, 0:1], scalar2=1.0 / 448.0, op0=ALU.max, op1=ALU.mult
+        )
+        amT = psum.tile([P, P], F32, tag="tp", bufs=4, name="amT")
+        nc.tensor.transpose(amT[:], amp[:, 0:1].to_broadcast([P, P]), ident_f[:])
+        amax = const.tile([P, 1], F32, name="amax")
+        nc.vector.tensor_reduce(out=amax[:], in_=amT[:], axis=AX.X, op=ALU.max)
+        rs = const.tile([P, 1], F32, name="rs")
+        nc.vector.reciprocal(out=rs[:], in_=amax[:])
+
+        o8s = []
+        for r in range(R):
+            o8 = const.tile([P, D], FP8, name="o8_%d" % r)
+            o8s.append(o8)
+
+        def cast_v(r, a, b):
+            nc.vector.tensor_scalar(
+                out=o8s[r][:, a:b], in0=ys[r][:, a:b], scalar1=rs[:, 0:1], scalar2=None, op0=ALU.mult,
+                saturate=False,
+            )
+
+        def cast_s(r, a, b):
+            nc.scalar.activation(
+                out=o8s[r][:, a:b], in_=ys[r][:, a:b], func=ACT.Identity, scale=rs[:, 0:1], bias=zero[:, 0:1],
+                saturate=False,
+            )
+
+        def store8(r):
+            nc.sync.dma_start(out=o1v[r // 2, :, r % 2, :], in_=o8s[r][:].bitcast(U8))
+
+        cast_v(0, 0, D)
+        store8(0)
+        cast_s(3, 0, D)
+        cast_v(1, 0, D)
+        store8(1)
+        store8(3)
+        cast_s(2, 704, D)
+        cast_v(2, 0, 704)
+        store8(2)

@@ -70,12 +70,11 @@ def tile_multiheadattentionunit_pa_kernel(tc, attn, Wo, bo, query_inputs, gamma,
         nc.vector.memset(one[:], 1.0)
         zero = const.tile([P, 1], F32, name="zero")
         nc.vector.memset(zero[:], 0.0)
-        warm = const.tile([P, 1], F32, name="warm")
-        nc.scalar.activation(out=warm[:], in_=one[:], func=ACT.Sqrt)
-
         braw = const.tile([P, P], BF16, name="braw")
         nc.vector.memset(braw[64:128, :], 0.0)
         nc.scalar.dma_start(out=braw[0:64, :], in_=bo.rearrange("h (c p) -> (h c) p", p=P))
+        warm = const.tile([P, 1], F32, name="warm")
+        nc.scalar.activation(out=warm[:], in_=one[:], func=ACT.Sqrt)
 
         for h in range(PRE):
             loads(h)
@@ -86,16 +85,21 @@ def tile_multiheadattentionunit_pa_kernel(tc, attn, Wo, bo, query_inputs, gamma,
         make_identity(nc, ident_f[:])
 
         NDC = D // P
-        bT = psum.tile([P, P], BF16, tag="tp", bufs=4, name="bT")
-        nc.tensor.transpose(bT[:], braw[:], ident_b[:])
         negb = const.tile([P, H * NDC], F32, name="negb")
-        nc.vector.tensor_scalar(out=negb[:], in0=bT[:, 0 : H * NDC], scalar1=-1.0, scalar2=None, op0=ALU.mult)
         posb = const.tile([P, H * NDC], F32, name="posb")
-        nc.vector.tensor_copy(out=posb[:], in_=bT[:, 0 : H * NDC])
         bsum = const.tile([P, NDC], F32, name="bsum")
-        nc.vector.tensor_reduce(
-            out=bsum[:], in_=posb[:].rearrange("p (h c) -> p c h", h=H), axis=AX.X, op=ALU.add
-        )
+
+        def bias_T():
+            bT = psum.tile([P, P], BF16, tag="mm", bufs=4, name="bT")
+            nc.tensor.transpose(bT[:], braw[:], ident_b[:])
+            return bT
+
+        def bias_V(bT):
+            nc.vector.tensor_scalar(out=negb[:], in0=bT[:, 0 : H * NDC], scalar1=-1.0, scalar2=None, op0=ALU.mult)
+            nc.vector.tensor_copy(out=posb[:], in_=bT[:, 0 : H * NDC])
+            nc.vector.tensor_reduce(
+                out=bsum[:], in_=posb[:].rearrange("p (h c) -> p c h", h=H), axis=AX.X, op=ALU.add
+            )
 
         qraw = const.tile([P, R, D], BF16, name="qraw")
         gam = const.tile([P, D], BF16, name="gam")
@@ -333,6 +337,7 @@ def tile_multiheadattentionunit_pa_kernel(tc, attn, Wo, bo, query_inputs, gamma,
 
         attn_T(0)
         attn_T(1)
+        bT0 = bias_T()
         attn_E(0)
         attn_E(1)
         for k in range(2):
@@ -344,6 +349,7 @@ def tile_multiheadattentionunit_pa_kernel(tc, attn, Wo, bo, query_inputs, gamma,
         icopy("V", 0, 1, 0, VB[0])
         icopy("S", 0, 1, VB[0], HD)
         wo_Q(0)
+        bias_V(bT0)
         attn_T(2)
         for i in range(4):
             mx(0, i)

@@ -23,7 +23,7 @@ R = NT // P
 NG = DV // 512
 HD = D // 2
 NU = 2 * H
-GC = 384
+GC = 352
 VA = (352, 176)
 VB = (352, 384)
 VA2 = 416

@@ -155,7 +155,10 @@ def tile_multiheadattentionunit_pa_kernel(tc, attn, Wo, bo, query_inputs, gamma,
             src = wraws[(h, g, half)][:, :, lo:hi].rearrange("p j d -> p d j")
             dst = wgrps[(k, g)][:, lo:hi, :]
             if eng == "V":
-                nc.vector.tensor_copy(out=dst, in_=src)
+                nc.vector.tensor_copy(
+                    out=wgrps[(k, g)][:, lo:hi, :].rearrange("p (c i) t -> p c t i", i=4),
+                    in_=wraws[(h, g, half)][:, :, lo:hi].rearrange("p t (c i) -> p c t i", i=4),
+                )
             elif eng == "S":
                 nc.scalar.copy(
                     out=wgrps[(k, g)][:, lo:hi, :].rearrange("p (c i) t -> p c t i", i=4),

@@ -180,7 +180,7 @@ def tile_multiheadattentionunit_pa_kernel(tc, attn, Wo, bo, query_inputs, gamma,
                 return
             code = stream.tile([P, NG, HD], U32, tag="wcode", bufs=3, name="wcode", align_bytes=64)
             scl = stream.tile([P, NG, HD], U8, tag="wscl", bufs=3, name="wscl", align_bytes=64)
-            for g in range(NG):
+            for g in ((1, 0) if k >= 2 else (0, 1)):
                 nc.vector.quantize_mx(
                     out=code[:, g, :].bitcast(FP8X4),
                     scales=scl[:, g, :],
@@ -280,19 +280,19 @@ def tile_multiheadattentionunit_pa_kernel(tc, attn, Wo, bo, query_inputs, gamma,
             mvs[r] = mv
 
         def v_vareps_bn(r):
-            nc.vector.tensor_scalar(
-                out=sts[r][:, 5:6], in0=mvs[r][:, 1:2], scalar1=float(D), scalar2=LN_EPS * D,
-                op0=ALU.mult, op1=ALU.add,
-            )
+            return
 
         def v_vareps(r):
-            nc.vector.tensor_scalar(
-                out=sts[r][:, 5:6], in0=sts[r][:, 3:4], scalar1=sts[r][:, 4:5], scalar2=LN_EPS * D,
-                op0=ALU.add, op1=ALU.add,
-            )
+            return
 
         def s_sqrt(r):
-            nc.scalar.activation(out=sts[r][:, 6:7], in_=sts[r][:, 5:6], func=ACT.Sqrt, scale=1.0 / D)
+            if r in mvs:
+                nc.scalar.activation(out=sts[r][:, 6:7], in_=mvs[r][:, 1:2], func=ACT.Sqrt, scale=1.0, bias=LN_EPS)
+            else:
+                nc.scalar.activation(
+                    out=sts[r][:, 5:6], in_=sts[r][:, 3:4], func=ACT.Identity, bias=sts[r][:, 4:5], scale=1.0
+                )
+                nc.scalar.activation(out=sts[r][:, 6:7], in_=sts[r][:, 5:6], func=ACT.Sqrt, scale=1.0 / D, bias=LN_EPS)
 
         def v_recip(r):
             nc.vector.reciprocal(out=sts[r][:, 7:8], in_=sts[r][:, 6:7])
@@ -421,7 +421,6 @@ def tile_multiheadattentionunit_pa_kernel(tc, attn, Wo, bo, query_inputs, gamma,
                 x_add(r, c)
 
         v_stats(0)
-        v_vareps_bn(0)
         s_sum(1, 1)
         s_negmean(1)
         s_sqrt(0)
@@ -435,7 +434,6 @@ def tile_multiheadattentionunit_pa_kernel(tc, attn, Wo, bo, query_inputs, gamma,
         v_center_gain(1, 1)
         v_scale_shift(0)
         s_square(1)
-        v_vareps(1)
         s_sum(3, 0)
         s_sqrt(1)
         s_sum(3, 1)
@@ -446,21 +444,19 @@ def tile_multiheadattentionunit_pa_kernel(tc, attn, Wo, bo, query_inputs, gamma,
         v_absmax(0)
         v_scale_shift(1)
         s_square(2)
-        v_vareps(2)
         s_sqrt(2)
+        s_square(3)
+        s_sqrt(3)
         v_center_gain(3, 0)
         v_recip(2)
         v_center_gain(3, 1)
+        v_recip(3)
         v_absmax(1)
         v_scale_shift(2)
-        s_square(3)
-        v_vareps(3)
-        s_sqrt(3)
-        v_absmax(2)
-        v_prevmax()
-        v_recip(3)
         v_scale_shift(3)
+        v_absmax(2)
         v_absmax(3)
+        v_prevmax()
 
         amp = const.tile([P, 1], F32, name="amp")
         nc.vector.tensor_scalar(

@@ -338,6 +338,15 @@ def tile_multiheadattentionunit_pa_kernel(tc, attn, Wo, bo, query_inputs, gamma,
                 out=am[:, r : r + 1], in_=ys[r][:], axis=AX.X, op=ALU.max, apply_absolute_value=True
             )
 
+        wz = const.tile([P, NT], BF16, name="wz")
+        nc.gpsimd.memset(wz[:], 0.0)
+        wp = psum.tile([P, NT], F32, tag="mm", bufs=4, name="wp")
+
+        def warm_pe(rhs, n):
+            for wi_ in range(n):
+                nc.tensor.matmul(out=wp[:], lhsT=ident_b[:], rhs=rhs, start=True, stop=True)
+
+        warm_pe(wz[:], 0)
         attn_T(0)
         attn_T(1)
         bT0 = bias_T()
@@ -351,6 +360,9 @@ def tile_multiheadattentionunit_pa_kernel(tc, attn, Wo, bo, query_inputs, gamma,
         wo_alloc(0, 1)
         icopy("V", 0, 1, 0, VB[0])
         icopy("S", 0, 1, VB[0], HD)
+        warm_pe(wgrps[(0, 0)][:, 0:P, :].rearrange("p d j -> p (d j)"), 3)
+        warm_pe(wgrps[(1, 0)][:, 0:P, :].rearrange("p d j -> p (d j)"), 3)
+        warm_pe(wgrps[(0, 1)][:, 0:P, :].rearrange("p d j -> p (d j)"), 3)
         wo_Q(0)
         bias_V(bT0)
         attn_T(2)

from contextlib import ExitStack

import concourse.mybir as mybir
from concourse.masks import make_identity

B, H, S, DV, D = 2, 8, 256, 1024, 1024
LN_EPS = 1e-3
FLOPS = 2 * B * H * S * DV * D

F32 = mybir.dt.float32
BF16 = mybir.dt.bfloat16
U32 = mybir.dt.uint32
U8 = mybir.dt.uint8
FP8X4 = mybir.dt.float8_e4m3fn_x4
FP8 = mybir.dt.float8_e4m3fn
ALU = mybir.AluOpType
ACT = mybir.ActivationFunctionType
AX = mybir.AxisListType

P = 128
NT = B * S
R = NT // P
NG = DV // 512
HD = D // 2
NU = 2 * H
GC = 352
VA = (352, 176)
VB = (352, 384)
VA2 = 416
ABUFS = 3
WBUFS = 6
PRE = 3
LE = 3


def tile_multiheadattentionunit_pa_kernel(tc, attn, Wo, bo, query_inputs, gamma, beta, out_0, out_1):
    nc = tc.nc
    with ExitStack() as ctx:
        const = ctx.enter_context(tc.tile_pool(name="const", bufs=1))
        stream = ctx.enter_context(tc.tile_pool(name="stream", bufs=2))
        psum = ctx.enter_context(tc.psum_pool(name="psum", bufs=4))
        ctx.enter_context(tc.manual_schedule())

        araws = {}
        wraws = {}

        def load_attn(h):
            araw = stream.tile([P, R, DV], BF16, tag="araw", bufs=ABUFS, name="araw")
            nc.sync.dma_start(
                out=araw[:].rearrange("p (b e) k -> p b (e k)", b=B),
                in_=attn[:, h].rearrange("b (p e) k -> p b (e k)", e=2),
            )
            for g in range(NG):
                araws[(h, g)] = araw[:, :, 512 * g : 512 * (g + 1)]

        def load_wo(h, g):
            wraw = stream.tile([P, 4, D], BF16, tag="wraw", bufs=WBUFS, name="wraw")
            nc.sync.dma_start(
                out=wraw[:], in_=Wo[h, 512 * g : 512 * (g + 1), :].rearrange("(p j) d -> p j d", j=4)
            )
            for hf in range(2):
                wraws[(h, g, hf)] = wraw[:, :, hf * HD : (hf + 1) * HD]

        def loads(h):
            load_attn(h)
            for g in ((1, 0) if h == 1 else (0, 1)):
                load_wo(h, g)

        one = const.tile([P, 1], F32, name="one")
        nc.vector.memset(one[:], 1.0)
        zero = const.tile([P, 1], F32, name="zero")
        nc.vector.memset(zero[:], 0.0)
        braw = const.tile([P, P], BF16, name="braw")
        nc.vector.memset(braw[64:128, :], 0.0)
        nc.scalar.dma_start(out=braw[0:64, :], in_=bo.rearrange("h (c p) -> (h c) p", p=P))
        warm = const.tile([P, 1], F32, name="warm")
        nc.scalar.activation(out=warm[:], in_=one[:], func=ACT.Sqrt)

        for h in range(PRE):
            loads(h)

        ident_b = const.tile([P, P], BF16, name="ident_b")
        make_identity(nc, ident_b[:])
        ident_f = const.tile([P, P], F32, name="ident_f")
        make_identity(nc, ident_f[:])

        NDC = D // P
        negb = const.tile([P, H * NDC], F32, name="negb")
        posb = const.tile([P, H * NDC], F32, name="posb")
        bsum = const.tile([P, NDC], F32, name="bsum")

        def bias_T():
            bT = psum.tile([P, P], BF16, tag="mm", bufs=4, name="bT")
            nc.tensor.transpose(bT[:], braw[:], ident_b[:])
            return bT

        def bias_V(bT):
            nc.vector.tensor_scalar(out=negb[:], in0=bT[:, 0 : H * NDC], scalar1=-1.0, scalar2=None, op0=ALU.mult)
            nc.vector.tensor_copy(out=posb[:], in_=bT[:, 0 : H * NDC])
            nc.vector.tensor_reduce(
                out=bsum[:], in_=posb[:].rearrange("p (h c) -> p c h", h=H), axis=AX.X, op=ALU.add
            )

        qraw = const.tile([P, R, D], BF16, name="qraw")
        gam = const.tile([P, D], BF16, name="gam")
        bet = const.tile([P, D], BF16, name="bet")

        tps = {}
        agrps = {}
        acodes = {}
        wgrps = {}
        wcodes = {}
        mms = {}

        def attn_T(a):
            if a >= NU:
                return
            h, g = a // 2, a % 2
            araw = araws[(h, g)]
            for r2 in range(2):
                tp = psum.tile([P, 2, 2, P], F32, tag="tp", bufs=4, name="tp")
                for rr in range(2):
                    words = araw[:, 2 * r2 + rr, :].bitcast(F32)
                    for u in range(2):
                        nc.tensor.transpose(tp[:, rr, u, :], words[:, u:256:2], ident_f[:])
                tps[(a, r2)] = tp

        def attn_E(a):
            if a >= NU:
                return
            h, g = a // 2, a % 2
            if g == 0:
                agrp = stream.tile([P, NG, 4 * NT], BF16, tag="agrp", bufs=2, name="agrp", align_bytes=64)
                agrps[h] = agrp
            gw = agrps[h][:, g, :].bitcast(F32).rearrange("p (r n u) -> p r n u", r=R, u=2)
            for r2 in range(2):
                nc.scalar.copy(
                    out=gw[:, 2 * r2 : 2 * r2 + 2, :, :], in_=tps[(a, r2)][:].rearrange("p r u n -> p r n u")
                )

        def attn_Q(h):
            if h >= H:
                return
            code = stream.tile([P, NG, NT], U32, tag="acode", bufs=2, name="acode", align_bytes=64)
            scl = stream.tile([P, NG, NT], U8, tag="ascl", bufs=2, name="ascl", align_bytes=64)
            nc.vector.quantize_mx(
                out=code[:].rearrange("p g n -> p (g n)").bitcast(FP8X4),
                scales=scl[:].rearrange("p g n -> p (g n)"),
                in_=agrps[h][:].rearrange("p g n -> p (g n)"),
            )
            acodes[h] = (code, scl)

        def icopy(eng, k, g, lo, hi):
            h, half = k // 2, k % 2
            src = wraws[(h, g, half)][:, :, lo:hi].rearrange("p j d -> p d j")
            dst = wgrps[(k, g)][:, lo:hi, :]
            if eng == "V":
                nc.vector.tensor_copy(
                    out=wgrps[(k, g)][:, lo:hi, :].rearrange("p (c i) t -> p c t i", i=4),
                    in_=wraws[(h, g, half)][:, :, lo:hi].rearrange("p t (c i) -> p c t i", i=4),
                )
            elif eng == "S":
                nc.scalar.copy(
                    out=wgrps[(k, g)][:, lo:hi, :].rearrange("p (c i) t -> p c t i", i=4),
                    in_=wraws[(h, g, half)][:, :, lo:hi].rearrange("p t (c i) -> p c t i", i=4),
                )
            else:
                nc.gpsimd.tensor_scalar(out=dst, in0=src, scalar1=1.0, scalar2=0.0, op0=ALU.mult, op1=ALU.add)

        def wo_alloc(k, g):
            if g == 0:
                wgrpa = stream.tile([P, HD, 4], BF16, tag="wgrpa", bufs=2, name="wgrpa", align_bytes=64)
                wgrps[(k, 0)] = wgrpa
            else:
                wgrpb = stream.tile([P, HD, 4], BF16, tag="wgrpb", bufs=1, name="wgrpb", align_bytes=64)
                wgrps[(k, 1)] = wgrpb

        def wo_Q(k):
            if k >= NU:
                return
            code = stream.tile([P, NG, HD], U32, tag="wcode", bufs=3, name="wcode", align_bytes=64)
            scl = stream.tile([P, NG, HD], U8, tag="wscl", bufs=3, name="wscl", align_bytes=64)
            for g in ((1, 0) if k >= 2 else (0, 1)):
                nc.vector.quantize_mx(
                    out=code[:, g, :].bitcast(FP8X4),
                    scales=scl[:, g, :],
                    in_=wgrps[(k, g)][:].rearrange("p d j -> p (d j)"),
                )
            wcodes[k] = (code, scl)

        accs = []
        for c in range(NDC):
            acc = const.tile([P, NT], F32, name="acc%d" % c)
            accs.append(acc)

        def mx(k, i):
            if k >= NU:
                return
            h = k // 2
            mm = psum.tile([P, NT], F32, tag=("tp" if k == NU - 1 else "mm"), bufs=4, name="mm")
            cols = slice(i * P, (i + 1) * P)
            ac, asc = acodes[h]
            wc, ws = wcodes[k]
            for g in range(NG):
                nc.tensor.matmul_mx(
                    out=mm[:],
                    lhsT=wc[:, g, cols].bitcast(FP8X4),
                    lhsT_scale=ws[:, g, cols],
                    rhs=ac[:, g, :].bitcast(FP8X4),
                    rhs_scale=asc[:, g, :],
                    start=(g == 0),
                    stop=(g == NG - 1),
                )
            mms[(k, i)] = mm

        def relu_add(k, i):
            h, half = k // 2, k % 2
            c = 4 * half + i
            nb = negb[:, h * NDC + c : h * NDC + c + 1]
            if h == 0:
                nc.vector.tensor_scalar(
                    out=accs[c][:], in0=mms[(k, i)][:], scalar1=nb, scalar2=bsum[:, c : c + 1],
                    op0=ALU.max, op1=ALU.add,
                )
            else:
                nc.vector.scalar_tensor_tensor(
                    out=accs[c][:], in0=mms[(k, i)][:], scalar=nb, in1=accs[c][:], op0=ALU.max, op1=ALU.add
                )

        xts = {}

        def x_open(r, hf):
            xt = psum.tile([P, HD], F32, tag=("mm" if r < 2 else "tp"), bufs=4, name="xt%d%d" % (r, hf))
            nc.tensor.matmul(
                out=xt[:], lhsT=ident_b[:], rhs=qraw[:, r, hf * HD : (hf + 1) * HD], start=True, stop=False
            )
            xts[(r, hf)] = xt

        def x_add(r, c):
            nc.tensor.matmul(
                out=xts[(r, c // 4)][:, (c % 4) * P : (c % 4 + 1) * P],
                lhsT=accs[c][:, r * P : (r + 1) * P],
                rhs=ident_f[:],
                is_transpose=True,
                start=False,
                stop=(c % 4 == 3),
            )

        sts = []
        for r in range(R):
            st = const.tile([P, 8], F32, name="st%d" % r)
            sts.append(st)

        def s_sum(r, hf):
            junk = stream.tile([P, HD], F32, tag="junk", bufs=2, name="junk")
            nc.scalar.activation(
                out=junk[:], in_=xts[(r, hf)][:], func=ACT.Identity, scale=-1.0 / D,
                accum_out=sts[r][:, hf : hf + 1],
            )

        def s_negmean(r):
            nc.scalar.activation(
                out=sts[r][:, 2:3], in_=sts[r][:, 0:1], func=ACT.Identity, bias=sts[r][:, 1:2], scale=1.0
            )

        def s_square(r):
            for hf in range(2):
                junk = stream.tile([P, HD], F32, tag="junk", bufs=2, name="junk")
                nc.scalar.activation(
                    out=junk[:], in_=xts[(r, hf)][:], func=ACT.Square, bias=sts[r][:, 2:3], scale=1.0,
                    accum_out=sts[r][:, 3 + hf : 4 + hf],
                )

        def v_stats(r):
            bst = const.tile([P, 2, 6], F32, name="bst%d" % r)
            for hf in range(2):
                nc.vector.bn_stats(out=bst[:, hf, :], in_=xts[(r, hf)][:])
            mv = const.tile([P, 2], F32, name="mv%d" % r)
            nc.vector.bn_aggr(out=mv[:], in_=bst[:].rearrange("p a b -> p (a b)"))
            mvs[r] = mv

        def v_vareps_bn(r):
            return

        def v_vareps(r):
            return

        def s_sqrt(r):
            if r in mvs:
                nc.scalar.activation(out=sts[r][:, 6:7], in_=mvs[r][:, 1:2], func=ACT.Sqrt, scale=1.0, bias=LN_EPS)
            else:
                nc.scalar.activation(
                    out=sts[r][:, 5:6], in_=sts[r][:, 3:4], func=ACT.Identity, bias=sts[r][:, 4:5], scale=1.0
                )
                nc.scalar.activation(out=sts[r][:, 6:7], in_=sts[r][:, 5:6], func=ACT.Sqrt, scale=1.0 / D, bias=LN_EPS)

        def v_recip(r):
            nc.vector.reciprocal(out=sts[r][:, 7:8], in_=sts[r][:, 6:7])

        t1s = {}
        ys = {}
        mvs = {}
        am = const.tile([P, R], F32, name="am")
        o0v = out_0.rearrange("b (p e) d -> b p e d", e=2)
        o1v = out_1.rearrange("b (p e) d -> b p e d", e=2)

        def v_center_gain(r, hf):
            if hf == 0:
                t1 = stream.tile([P, D], F32, tag="t1", bufs=4, name="t1")
                t1s[r] = t1
            cols = slice(hf * HD, (hf + 1) * HD)
            if r in mvs:
                nc.vector.scalar_tensor_tensor(
                    out=t1s[r][:, cols], in0=xts[(r, hf)][:], scalar=mvs[r][:, 0:1], in1=gam[:, cols],
                    op0=ALU.subtract, op1=ALU.mult,
                )
            else:
                nc.vector.scalar_tensor_tensor(
                    out=t1s[r][:, cols], in0=xts[(r, hf)][:], scalar=sts[r][:, 2:3], in1=gam[:, cols],
                    op0=ALU.add, op1=ALU.mult,
                )

        def v_scale_shift(r):
            y = const.tile([P, D], F32, name="y%d" % r)
            nc.vector.scalar_tensor_tensor(
                out=y[:], in0=t1s[r][:], scalar=sts[r][:, 7:8], in1=bet[:], op0=ALU.mult, op1=ALU.add
            )
            nc.sync.dma_start(out=o0v[r // 2, :, r % 2, :], in_=y[:])
            ys[r] = y

        pm = const.tile([P, 1], F32, name="pm")

        def v_prevmax():
            nc.vector.tensor_reduce(out=pm[:], in_=am[:, 0 : R - 1], axis=AX.X, op=ALU.max)

        def v_absmax(r):
            nc.vector.tensor_reduce(
                out=am[:, r : r + 1], in_=ys[r][:], axis=AX.X, op=ALU.max, apply_absolute_value=True
            )

        wz = const.tile([P, NT], BF16, name="wz")
        nc.gpsimd.memset(wz[:], 0.0)
        wp = psum.tile([P, NT], F32, tag="mm", bufs=4, name="wp")

        def warm_pe(rhs, n):
            for wi_ in range(n):
                nc.tensor.matmul(out=wp[:], lhsT=ident_b[:], rhs=rhs, start=True, stop=True)

        warm_pe(wz[:], 0)
        attn_T(0)
        attn_T(1)
        bT0 = bias_T()
        attn_E(0)
        attn_E(1)
        for k in range(2):
            wo_alloc(k, 0)
            icopy("V", k, 0, 0, VA[k])
            icopy("S", k, 0, VA[k], HD)
        attn_Q(0)
        wo_alloc(0, 1)
        icopy("V", 0, 1, 0, VB[0])
        icopy("S", 0, 1, VB[0], HD)
        warm_pe(wgrps[(0, 0)][:, 0:P, :].rearrange("p d j -> p (d j)"), 3)
        warm_pe(wgrps[(1, 0)][:, 0:P, :].rearrange("p d j -> p (d j)"), 3)
        warm_pe(wgrps[(0, 1)][:, 0:P, :].rearrange("p d j -> p (d j)"), 3)
        wo_Q(0)
        bias_V(bT0)
        attn_T(2)
        for i in range(4):
            mx(0, i)
        attn_T(3)
        wo_alloc(1, 1)
        icopy("V", 1, 1, 0, VB[1])
        if VB[1] < HD:
            icopy("S", 1, 1, VB[1], HD)
        attn_E(2)

        for s in range(NU):
            if s % 2 == 0 and s // 2 + PRE < H:
                loads(s // 2 + PRE)
            if s == 10:
                for b in range(B):
                    nc.sync.dma_start(
                        out=qraw[:, 2 * b : 2 * b + 2, :], in_=query_inputs[b].rearrange("(p e) d -> p e d", e=2)
                    )
                nc.sync.dma_start(out=gam[:], in_=gamma.partition_broadcast(P))
                nc.sync.dma_start(out=bet[:], in_=beta.partition_broadcast(P))
            wo_Q(s + 1)
            if s == NU - 2:
                for i in range(4):
                    mx(s + 1, i)
            k = s + 2
            if k < NU:
                wo_alloc(k, 0)
                wo_alloc(k, 1)
                icopy("G", k, 1, 0, GC)
                if s == 0:
                    icopy("S", k, 1, GC, HD)
                    attn_E(s + LE)
                    icopy("S", k, 0, VA2, HD)
                else:
                    icopy("S", k, 0, 0, HD)
                    attn_E(s + LE)
                    icopy("S", k, 1, GC, HD)
            if s == NU - 1:
                s_sum(1, 0)
            for i in range(4):
                relu_add(s, i)
                if s < NU - 2:
                    if i == 3:
                        attn_T(s + LE + 1)
                    mx(s + 1, i)
                elif s == NU - 2:
                    x_open(i // 2, i % 2)
                    x_add(0, i)
                    if i == 2:
                        x_add(1, 0)
                        x_add(1, 1)
                    if i >= 2:
                        x_add(1, i)
                else:
                    x_add(0, 4 + i)
                    x_add(1, 4 + i)
            if s % 2 == 0:
                attn_Q(s // 2 + 1)
            if s == 0:
                icopy("V", k, 0, 0, VA2)

        for r in range(2, R):
            x_open(r, 0)
            x_open(r, 1)
            for c in range(NDC):
                x_add(r, c)

        v_stats(0)
        s_sum(1, 1)
        s_negmean(1)
        s_sqrt(0)
        v_center_gain(0, 0)
        v_center_gain(0, 1)
        s_sum(2, 0)
        s_sum(2, 1)
        s_negmean(2)
        v_center_gain(1, 0)
        v_recip(0)
        v_center_gain(1, 1)
        v_scale_shift(0)
        s_square(1)
        s_sum(3, 0)
        s_sqrt(1)
        s_sum(3, 1)
        s_negmean(3)
        v_center_gain(2, 0)
        v_recip(1)
        v_center_gain(2, 1)
        v_absmax(0)
        v_scale_shift(1)
        s_square(2)
        s_sqrt(2)
        s_square(3)
        s_sqrt(3)
        v_center_gain(3, 0)
        v_recip(2)
        v_center_gain(3, 1)
        v_recip(3)
        v_absmax(1)
        v_scale_shift(2)
        v_scale_shift(3)
        v_absmax(2)
        v_absmax(3)
        v_prevmax()

        amp = const.tile([P, 1], F32, name="amp")
        nc.vector.tensor_scalar(
            out=amp[:], in0=am[:, R - 1 : R], scalar1=pm[:, 0:1], scalar2=1.0 / 448.0, op0=ALU.max, op1=ALU.mult
        )
        amT = psum.tile([P, P], F32, tag="tp", bufs=4, name="amT")
        nc.tensor.transpose(amT[:], amp[:, 0:1].to_broadcast([P, P]), ident_f[:])
        amax = const.tile([P, 1], F32, name="amax")
        nc.vector.tensor_reduce(out=amax[:], in_=amT[:], axis=AX.X, op=ALU.max)
        rs = const.tile([P, 1], F32, name="rs")
        nc.vector.reciprocal(out=rs[:], in_=amax[:])

        o8s = []
        for r in range(R):
            o8 = const.tile([P, D], FP8, name="o8_%d" % r)
            o8s.append(o8)

        def cast_v(r, a, b):
            nc.vector.tensor_scalar(
                out=o8s[r][:, a:b], in0=ys[r][:, a:b], scalar1=rs[:, 0:1], scalar2=None, op0=ALU.mult,
                saturate=False,
            )

        def cast_s(r, a, b):
            nc.scalar.activation(
                out=o8s[r][:, a:b], in_=ys[r][:, a:b], func=ACT.Identity, scale=rs[:, 0:1], bias=zero[:, 0:1],
                saturate=False,
            )

        def store8(r):
            nc.sync.dma_start(out=o1v[r // 2, :, r % 2, :], in_=o8s[r][:].bitcast(U8))

        cast_v(0, 0, D)
        store8(0)
        cast_s(3, 0, D)
        cast_v(1, 0, D)
        store8(1)
        store8(3)
        cast_s(2, 704, D)
        cast_v(2, 0, 704)
        store8(2)
